import numpy as np
import ml_dtypes


def mxq(x, axis, fmt="e4m3"):
    dtype, down = {"e4m3": (ml_dtypes.float8_e4m3fn, 7), "e5m2": (ml_dtypes.float8_e5m2, 14)}[fmt]
    v = np.moveaxis(np.asarray(x, np.float32).astype(ml_dtypes.bfloat16).astype(np.float64), axis, -1)
    blocks = v.reshape(v.shape[:-1] + (-1, 32))
    amax = np.abs(blocks).max(-1, keepdims=True)
    byte = np.maximum(np.where(amax > 0, np.frexp(amax)[1] - 1 + 127, 0) - down, 1)
    scale = np.exp2(byte - 127.0)
    codes = (blocks / scale).astype(np.float32).astype(dtype).astype(np.float64)
    return np.moveaxis((codes * scale).reshape(v.shape), -1, axis)


WIDE = False


def mx_kscale(k):
    if not WIDE:
        return np.ones(k)
    levels = np.array([10, -10, 5, -5, 0])
    a = np.random.permutation(np.resize(levels, k // 512 * 4)).reshape(k // 512, 4)
    idx = np.arange(k)
    return np.exp2(a[idx // 512, idx % 128 // 32])


BF16 = ml_dtypes.bfloat16


def bf(x):
    return np.asarray(x, np.float32).astype(BF16)


def f64(x):
    return np.asarray(x).astype(np.float64)


E2M1 = np.array([0.0, 0.5, 1.0, 1.5, 2.0, 3.0, 4.0, 6.0, -0.0, -0.5, -1.0, -1.5, -2.0, -3.0, -4.0, -6.0])


def pack_weight(w, fmt):
    k, n = w.shape
    w = f64(bf(w)).reshape(k // 32, 32, n)
    amax = np.abs(w).max(1)
    if fmt == "e4m3":
        byte = np.frexp(amax)[1] - 1 + 127 - 7
    else:
        mant, ex = np.frexp(amax / 6.0)
        byte = np.where(mant > 0.5, ex, ex - 1) + 127
    byte = np.clip(np.where(amax > 0, byte, 1), 1, 254)
    scaled = (w * np.exp2(127.0 - byte)[:, None, :]).reshape(k, n).astype(np.float32)
    by_word = np.ascontiguousarray(scaled.reshape(k // 512, 128, 4, n).transpose(0, 1, 3, 2))
    if fmt == "e4m3":
        words = by_word.astype(ml_dtypes.float8_e4m3fn).view(np.uint8)
    else:
        c = by_word.astype(ml_dtypes.float4_e2m1fn).view(np.uint8) & 0xF
        words = c[..., 0::2] | (c[..., 1::2] << 4)
    return np.ascontiguousarray(words), np.ascontiguousarray(byte.astype(np.uint8).reshape(k // 512, 16, n))


def unpack_weight(words, scales, fmt):
    g, p, n, _ = words.shape
    if fmt == "e4m3":
        vals = np.ascontiguousarray(words).view(ml_dtypes.float8_e4m3fn).astype(np.float64)
    else:
        nib = np.empty((g, p, n, 4), np.uint8)
        nib[..., 0::2] = words & 0xF
        nib[..., 1::2] = words >> 4
        vals = E2M1[nib]
    vals = vals * np.repeat(np.exp2(scales.astype(np.float64) - 127.0), 8, axis=1)[..., None]
    return vals.transpose(0, 1, 3, 2).reshape(g * 512, n)


B, D_IN, D_OUT = 1024, 1024, 1024
FMT = "e4m3"


def sigmoid(v):
    return 1.0 / (1.0 + np.exp(-v))


def setup_inputs():
    s, t = mx_kscale(D_IN), mx_kscale(D_OUT)

    def wx():
        return pack_weight(np.random.standard_normal((D_IN, D_OUT)) / np.sqrt(D_IN) / s[:, None], FMT)

    def wh():
        return pack_weight(np.random.standard_normal((D_OUT, D_OUT)) / np.sqrt(D_OUT) / t[:, None], FMT)

    x = bf(np.random.standard_normal((B, D_IN)) * s)
    hist = bf(np.random.standard_normal((B, D_OUT)) * t)
    Wix_words, Wix_scales = wx()
    Wih_words, Wih_scales = wh()
    b_i = bf(np.random.standard_normal(D_OUT) * 0.3)
    Wcx_words, Wcx_scales = wx()
    Wch_words, Wch_scales = wh()
    b_c = bf(np.random.standard_normal(D_OUT) * 0.3)
    return {"x": x,
            "hist": hist,
            "Wix_words": Wix_words, "Wix_scales": Wix_scales,
            "Wih_words": Wih_words, "Wih_scales": Wih_scales,
            "b_i": b_i,
            "Wcx_words": Wcx_words, "Wcx_scales": Wcx_scales,
            "Wch_words": Wch_words, "Wch_scales": Wch_scales,
            "b_c": b_c}


def reference(x, hist, Wix_words, Wix_scales, Wih_words, Wih_scales, b_i, Wcx_words, Wcx_scales, Wch_words, Wch_scales, b_c):
    xq = mxq(f64(x), 1, "e4m3")
    hq = mxq(f64(hist), 1, "e4m3")
    i = sigmoid((xq @ unpack_weight(Wix_words, Wix_scales, FMT)) + (hq @ unpack_weight(Wih_words, Wih_scales, FMT)) + f64(b_i))
    g = np.tanh((xq @ unpack_weight(Wcx_words, Wcx_scales, FMT)) + (hq @ unpack_weight(Wch_words, Wch_scales, FMT)) + f64(b_c))
    return i * g

@@ -1,0 +1,185 @@
+from contextlib import ExitStack
+
+import concourse.masks as masks
+import concourse.mybir as mybir
+
+F32 = mybir.dt.float32
+BF16 = mybir.dt.bfloat16
+I32 = mybir.dt.int32
+U32 = mybir.dt.uint32
+U8 = mybir.dt.uint8
+FP8X4 = mybir.dt.float8_e4m3fn_x4
+ACT = mybir.ActivationFunctionType
+ALU = mybir.AluOpType
+
+P = 128
+PACK = 4
+K_PASS = P * PACK
+TOKENS = 1024
+K_SOURCE = 1024
+N_OUT = 1024
+TILES = TOKENS // P
+PAIRS = TILES // 2
+GROUPS = K_SOURCE // K_PASS
+BANK = 512
+HALVES = N_OUT // BANK
+WORDS = K_PASS // 2
+RUN = 4
+
+FLOPS = 2 * TOKENS * (2 * K_SOURCE) * (2 * N_OUT)
+
+
+def tile_lstmmirrored_pa_kernel(
+    tc, x, hist, Wix_words, Wix_scales, Wih_words, Wih_scales, b_i,
+    Wcx_words, Wcx_scales, Wch_words, Wch_scales, b_c, out,
+):
+    nc = tc.nc
+    weight_words = ((Wix_words, Wih_words), (Wcx_words, Wch_words))
+    weight_scales = ((Wix_scales, Wih_scales), (Wcx_scales, Wch_scales))
+    biases = (b_i, b_c)
+    gate_function = (ACT.Sigmoid, ACT.Tanh)
+
+    source_view = [a.rearrange("(p t) k -> p t k", t=TILES) for a in (x, hist)]
+    out_view = out.rearrange("(p t) n -> p t n", t=TILES)
+
+    with ExitStack() as ctx:
+        keep = ctx.enter_context(tc.tile_pool(name="keep", bufs=1))
+        stage = ctx.enter_context(tc.tile_pool(name="stage", bufs=3))
+        gates = ctx.enter_context(tc.tile_pool(name="gates", bufs=6))
+        psum = ctx.enter_context(tc.psum_pool(name="psum", bufs=8))
+
+        warm = keep.tile([P, 1], F32, name="warm")
+        nc.vector.memset(warm[:], 0.0)
+        nc.scalar.activation(out=warm[:], in_=warm[:], func=ACT.Sigmoid)
+
+        w_planes = keep.tile([P, GROUPS, N_OUT], U8, name="w_planes", align_bytes=64)
+        nc.vector.memset(w_planes[:].rearrange("p g n -> p (g n)").bitcast(I32), 0)
+
+        bias_rows = keep.tile([P, 2, N_OUT], BF16, name="bias_rows")
+        nc.vector.memset(bias_rows[:].rearrange("p a n -> p (a n)").bitcast(I32), 0)
+        ones = keep.tile([P, P], BF16, name="ones")
+        nc.vector.memset(ones[:], 1.0)
+        identity = keep.tile([P, P], F32, name="identity")
+        masks.make_identity(nc, identity[:])
+
+        for gate in range(2):
+            nc.gpsimd.dma_start(out=bias_rows[0:1, gate, :], in_=biases[gate].unsqueeze(0))
+
+        raw = [[None] * PAIRS for source in range(2)]
+        for pair in range(PAIRS):
+            for source in range(2):
+                raw[source][pair] = keep.tile([P, 2, K_SOURCE], BF16, name="raw_%d_%d" % (source, pair))
+                nc.sync.dma_start(
+                    out=raw[source][pair][:], in_=source_view[source][:, 2 * pair : 2 * pair + 2, :]
+                )
+            gate, source = divmod(pair, 2)
+            scale_words = weight_scales[gate][source].bitcast(I32)
+            for r in range(4):
+                nc.sync.dma_start(
+                    out=w_planes[4 * pair + r : P : 32, :, :].bitcast(I32),
+                    in_=scale_words[:, r : 16 : 4, :].rearrange("g q n -> q g n"),
+                )
+
+        w_codes = [[[None] * HALVES for source in range(2)] for gate in range(2)]
+        for half in range(HALVES):
+            for gate in range(2):
+                for source in range(2):
+                    codes = keep.tile(
+                        [P, GROUPS, BANK], U32, name="w_codes_%d_%d_%d" % (gate, source, half), align_bytes=64
+                    )
+                    by_partition = weight_words[gate][source].rearrange("g p n t -> p g (n t)")
+                    nc.sync.dma_start(
+                        out=codes[:].bitcast(I32),
+                        in_=by_partition[:, :, PACK * BANK * half : PACK * BANK * (half + 1)].bitcast(I32),
+                    )
+                    w_codes[gate][source][half] = codes
+
+        a_codes = [[None] * PAIRS for source in range(2)]
+        a_planes = [[None] * PAIRS for source in range(2)]
+
+        def transpose_block(source, pair):
+            grouped = stage.tile([P, 2, GROUPS, P, PACK], BF16, name="grouped", align_bytes=64)
+            for i in range(2):
+                words = raw[source][pair][:, i, :].bitcast(F32)
+                flipped = psum.tile([P, GROUPS, 2, P], F32, name="flipped", tag="bank")
+                for g in range(GROUPS):
+                    for u in range(2):
+                        nc.tensor.transpose(
+                            flipped[:, g, u, :], words[:, WORDS * g + u : WORDS * (g + 1) : 2], identity[:]
+                        )
+                copy = nc.scalar.copy if i == 0 else nc.vector.tensor_copy
+                copy(out=grouped[:, i].bitcast(F32), in_=flipped[:].rearrange("p g u r -> p g r u"))
+            return grouped
+
+        def quantise_block(source, pair, grouped):
+            a_codes[source][pair] = keep.tile(
+                [P, 2, GROUPS, P], U32, name="a_codes_%d_%d" % (source, pair), align_bytes=64
+            )
+            a_planes[source][pair] = keep.tile(
+                [P, 2, GROUPS, P], U8, name="a_planes_%d_%d" % (source, pair), align_bytes=64
+            )
+            nc.vector.quantize_mx(
+                out=a_codes[source][pair][:].rearrange("p i g r -> p (i g r)").bitcast(FP8X4),
+                scales=a_planes[source][pair][:].rearrange("p i g r -> p (i g r)"),
+                in_=grouped[:].rearrange("p i g r t -> p (i g r t)"),
+            )
+
+        blocks = [(source, pair) for pair in range(PAIRS) for source in range(2)]
+        copied = None
+        for source, pair in blocks:
+            grouped = transpose_block(source, pair)
+            if copied is not None:
+                quantise_block(*copied)
+            copied = (source, pair, grouped)
+        quantise_block(*copied)
+
+        bias_all = keep.tile([P, 2, N_OUT], F32, name="bias_all")
+        for gate in range(2):
+            for half in range(HALVES):
+                columns = slice(BANK * half, BANK * (half + 1))
+                spread = psum.tile([P, BANK], F32, name="spread", tag="bank")
+                nc.tensor.matmul(spread[:], lhsT=ones[:], rhs=bias_rows[:, gate, columns], start=True, stop=True)
+                copy = nc.scalar.copy if gate == 0 else nc.vector.tensor_copy
+                copy(out=bias_all[:, gate, columns], in_=spread[:])
+
+        def gate_values(half, gate, tile_index):
+            pair, i = divmod(tile_index, 2)
+            columns = slice(BANK * half, BANK * (half + 1))
+            acc = psum.tile([P, BANK], F32, name="acc", tag="bank")
+            for source in range(2):
+                for g in range(GROUPS):
+                    nc.tensor.matmul_mx(
+                        out=acc[:],
+                        lhsT=a_codes[source][pair][:, i, g, :].bitcast(FP8X4),
+                        lhsT_scale=a_planes[source][pair][:, i, g, :],
+                        rhs=w_codes[gate][source][half][:, g, :].bitcast(FP8X4),
+                        rhs_scale=w_planes[4 * (2 * gate + source) : P, g, columns],
+                        start=(source == 0 and g == 0),
+                        stop=(source == 1 and g == GROUPS - 1),
+                    )
+            values = gates.tile([P, BANK], F32, name="values_%d" % gate)
+            nc.vector.tensor_tensor(out=values[:], in0=acc[:], in1=bias_all[:, gate, columns], op=ALU.add)
+            nc.scalar.activation(out=values[:], in_=values[:], func=gate_function[gate])
+            return values
+
+        def store_product(half, tile_index, input_gate, candidate):
+            nc.vector.tensor_tensor(out=candidate[:], in0=input_gate[:], in1=candidate[:], op=ALU.mult)
+            nc.sync.dma_start(
+                out=out_view[:, tile_index, BANK * half : BANK * (half + 1)], in_=candidate[:]
+            )
+
+        input_gates = [None] * TILES
+        finished = None
+        for half in range(HALVES):
+            for first in range(0, TILES, RUN):
+                for gate in range(2):
+                    for tile_index in range(first, first + RUN):
+                        values = gate_values(half, gate, tile_index)
+                        if finished is not None:
+                            store_product(*finished)
+                            finished = None
+                        if gate == 0:
+                            input_gates[tile_index] = values
+                        else:
+                            finished = (half, tile_index, input_gates[tile_index], values)
+        store_product(*finished)

@@ -24,7 +24,7 @@ GROUPS = K_SOURCE // K_PASS
 BANK = 512
 HALVES = N_OUT // BANK
 WORDS = K_PASS // 2
-RUN = 4
+WARM_UP = 5
 
 FLOPS = 2 * TOKENS * (2 * K_SOURCE) * (2 * N_OUT)
 
@@ -44,55 +44,75 @@ def tile_lstmmirrored_pa_kernel(
 
     with ExitStack() as ctx:
         keep = ctx.enter_context(tc.tile_pool(name="keep", bufs=1))
-        stage = ctx.enter_context(tc.tile_pool(name="stage", bufs=3))
+        stage = ctx.enter_context(tc.tile_pool(name="stage", bufs=4))
         gates = ctx.enter_context(tc.tile_pool(name="gates", bufs=6))
         psum = ctx.enter_context(tc.psum_pool(name="psum", bufs=8))
+        ctx.enter_context(tc.manual_schedule(engines={mybir.EngineType.PE}))
+
+        ones = keep.tile([P, BANK], BF16, name="ones")
+        nc.vector.memset(ones[:], 1.0)
+        bias_rows = keep.tile([P, 2, N_OUT], BF16, name="bias_rows")
+        nc.vector.memset(bias_rows[:].rearrange("p a n -> p (a n)").bitcast(I32), 0)
+        for gate in range(2):
+            nc.scalar.dma_start(out=bias_rows[0:1, gate, :], in_=biases[gate].unsqueeze(0))
 
         warm = keep.tile([P, 1], F32, name="warm")
         nc.vector.memset(warm[:], 0.0)
         nc.scalar.activation(out=warm[:], in_=warm[:], func=ACT.Sigmoid)
 
-        w_planes = keep.tile([P, GROUPS, N_OUT], U8, name="w_planes", align_bytes=64)
-        nc.vector.memset(w_planes[:].rearrange("p g n -> p (g n)").bitcast(I32), 0)
+        w_planes = [[None] * 2 for gate in range(2)]
+        for gate in range(2):
+            for source in range(2):
+                planes = keep.tile([P, GROUPS, N_OUT], U8, name="w_planes_%d_%d" % (gate, source), align_bytes=64)
+                nc.vector.memset(planes[:].rearrange("p g n -> p (g n)").bitcast(I32), 0)
+                w_planes[gate][source] = planes
 
-        bias_rows = keep.tile([P, 2, N_OUT], BF16, name="bias_rows")
-        nc.vector.memset(bias_rows[:].rearrange("p a n -> p (a n)").bitcast(I32), 0)
-        ones = keep.tile([P, P], BF16, name="ones")
-        nc.vector.memset(ones[:], 1.0)
         identity = keep.tile([P, P], F32, name="identity")
         masks.make_identity(nc, identity[:])
 
-        for gate in range(2):
-            nc.gpsimd.dma_start(out=bias_rows[0:1, gate, :], in_=biases[gate].unsqueeze(0))
 
         raw = [[None] * PAIRS for source in range(2)]
-        for pair in range(PAIRS):
+        w_codes = [[[None] * HALVES for source in range(2)] for gate in range(2)]
+
+        def load_activations(pair):
             for source in range(2):
                 raw[source][pair] = keep.tile([P, 2, K_SOURCE], BF16, name="raw_%d_%d" % (source, pair))
                 nc.sync.dma_start(
                     out=raw[source][pair][:], in_=source_view[source][:, 2 * pair : 2 * pair + 2, :]
                 )
-            gate, source = divmod(pair, 2)
+
+        def load_scales(gate, source):
             scale_words = weight_scales[gate][source].bitcast(I32)
             for r in range(4):
                 nc.sync.dma_start(
-                    out=w_planes[4 * pair + r : P : 32, :, :].bitcast(I32),
+                    out=w_planes[gate][source][r : P : 32, :, :].bitcast(I32),
                     in_=scale_words[:, r : 16 : 4, :].rearrange("g q n -> q g n"),
                 )
 
-        w_codes = [[[None] * HALVES for source in range(2)] for gate in range(2)]
-        for half in range(HALVES):
-            for gate in range(2):
-                for source in range(2):
-                    codes = keep.tile(
-                        [P, GROUPS, BANK], U32, name="w_codes_%d_%d_%d" % (gate, source, half), align_bytes=64
-                    )
-                    by_partition = weight_words[gate][source].rearrange("g p n t -> p g (n t)")
-                    nc.sync.dma_start(
-                        out=codes[:].bitcast(I32),
-                        in_=by_partition[:, :, PACK * BANK * half : PACK * BANK * (half + 1)].bitcast(I32),
-                    )
-                    w_codes[gate][source][half] = codes
+        def load_codes(gate, half):
+            for source in range(2):
+                codes = keep.tile(
+                    [P, GROUPS, BANK], U32, name="w_codes_%d_%d_%d" % (gate, source, half), align_bytes=64
+                )
+                by_partition = weight_words[gate][source].rearrange("g p n t -> p g (n t)")
+                nc.sync.dma_start(
+                    out=codes[:].bitcast(I32),
+                    in_=by_partition[:, :, PACK * BANK * half : PACK * BANK * (half + 1)].bitcast(I32),
+                )
+                w_codes[gate][source][half] = codes
+
+        load_activations(0)
+        load_scales(0, 0)
+        load_activations(1)
+        load_scales(0, 1)
+        load_codes(0, 0)
+        load_scales(1, 0)
+        load_codes(1, 0)
+        load_scales(1, 1)
+        load_activations(2)
+        load_activations(3)
+        load_codes(0, 1)
+        load_codes(1, 1)
 
         a_codes = [[None] * PAIRS for source in range(2)]
         a_planes = [[None] * PAIRS for source in range(2)]
@@ -124,62 +144,89 @@ def tile_lstmmirrored_pa_kernel(
                 in_=grouped[:].rearrange("p i g r t -> p (i g r t)"),
             )
 
-        blocks = [(source, pair) for pair in range(PAIRS) for source in range(2)]
-        copied = None
-        for source, pair in blocks:
-            grouped = transpose_block(source, pair)
-            if copied is not None:
-                quantise_block(*copied)
-            copied = (source, pair, grouped)
-        quantise_block(*copied)
-
         bias_all = keep.tile([P, 2, N_OUT], F32, name="bias_all")
-        for gate in range(2):
+
+        def spread_bias(gate):
             for half in range(HALVES):
                 columns = slice(BANK * half, BANK * (half + 1))
                 spread = psum.tile([P, BANK], F32, name="spread", tag="bank")
-                nc.tensor.matmul(spread[:], lhsT=ones[:], rhs=bias_rows[:, gate, columns], start=True, stop=True)
-                copy = nc.scalar.copy if gate == 0 else nc.vector.tensor_copy
+                nc.tensor.matmul(
+                    spread[:], lhsT=ones[:, 0:P], rhs=bias_rows[:, gate, columns], start=True, stop=True
+                )
+                copy = nc.scalar.copy if half == 0 else nc.vector.tensor_copy
                 copy(out=bias_all[:, gate, columns], in_=spread[:])
 
-        def gate_values(half, gate, tile_index):
-            pair, i = divmod(tile_index, 2)
+        def gate_values(half, gate, pair):
             columns = slice(BANK * half, BANK * (half + 1))
-            acc = psum.tile([P, BANK], F32, name="acc", tag="bank")
+            accs = []
+            for i in range(2):
+                acc = psum.tile([P, BANK], F32, name="acc", tag="bank")
+                accs.append(acc)
             for source in range(2):
-                for g in range(GROUPS):
-                    nc.tensor.matmul_mx(
-                        out=acc[:],
-                        lhsT=a_codes[source][pair][:, i, g, :].bitcast(FP8X4),
-                        lhsT_scale=a_planes[source][pair][:, i, g, :],
-                        rhs=w_codes[gate][source][half][:, g, :].bitcast(FP8X4),
-                        rhs_scale=w_planes[4 * (2 * gate + source) : P, g, columns],
-                        start=(source == 0 and g == 0),
-                        stop=(source == 1 and g == GROUPS - 1),
-                    )
-            values = gates.tile([P, BANK], F32, name="values_%d" % gate)
-            nc.vector.tensor_tensor(out=values[:], in0=acc[:], in1=bias_all[:, gate, columns], op=ALU.add)
-            nc.scalar.activation(out=values[:], in_=values[:], func=gate_function[gate])
-            return values
+                for i in range(2):
+                    for g in range(GROUPS):
+                        nc.tensor.matmul_mx(
+                            out=accs[i][:],
+                            lhsT=a_codes[source][pair][:, i, g, :].bitcast(FP8X4),
+                            lhsT_scale=a_planes[source][pair][:, i, g, :],
+                            rhs=w_codes[gate][source][half][:, g, :].bitcast(FP8X4),
+                            rhs_scale=w_planes[gate][source][:, g, columns],
+                            start=(source == 0 and g == 0),
+                            stop=(source == 1 and g == GROUPS - 1),
+                        )
+            pair_values = []
+            for i in range(2):
+                values = gates.tile([P, BANK], F32, name="values_%d" % gate)
+                nc.vector.tensor_tensor(out=values[:], in0=accs[i][:], in1=bias_all[:, gate, columns], op=ALU.add)
+                nc.scalar.activation(out=values[:], in_=values[:], func=gate_function[gate])
+                pair_values.append(values)
+            return pair_values
 
-        def store_product(half, tile_index, input_gate, candidate):
-            nc.vector.tensor_tensor(out=candidate[:], in0=input_gate[:], in1=candidate[:], op=ALU.mult)
-            nc.sync.dma_start(
-                out=out_view[:, tile_index, BANK * half : BANK * (half + 1)], in_=candidate[:]
-            )
+        def store_products(half, pair, input_gates, candidates):
+            for i in range(2):
+                nc.vector.tensor_tensor(out=candidates[i][:], in0=input_gates[i][:], in1=candidates[i][:], op=ALU.mult)
+                nc.sync.dma_start(
+                    out=out_view[:, 2 * pair + i, BANK * half : BANK * (half + 1)], in_=candidates[i][:]
+                )
 
-        input_gates = [None] * TILES
+        def keep_busy(count):
+            idle = psum.tile([P, BANK], F32, name="idle", tag="bank")
+            for n in range(count):
+                nc.tensor.matmul(idle[:], lhsT=ones[:, 0:P], rhs=ones[:], start=True, stop=True)
+
+        keep_busy(WARM_UP)
+        grouped_x = transpose_block(0, 0)
+        spread_bias(0)
+        grouped_h = transpose_block(1, 0)
+        quantise_block(0, 0, grouped_x)
+        spread_bias(1)
+        grouped_x = transpose_block(0, 1)
+        quantise_block(1, 0, grouped_h)
+        keep_busy(2)
+        grouped_h = transpose_block(1, 1)
+        quantise_block(0, 1, grouped_x)
+        quantise_block(1, 1, grouped_h)
+
+        jobs = [(0, 0, 0), (0, 0, 1), (0, 1, 0), (0, 1, 1), (0, 0, 2), (0, 1, 2), (0, 0, 3), (0, 1, 3)]
+        for pair in range(PAIRS):
+            for gate in range(2):
+                jobs.append((1, gate, pair))
+
+        input_gates = {}
         finished = None
-        for half in range(HALVES):
-            for first in range(0, TILES, RUN):
-                for gate in range(2):
-                    for tile_index in range(first, first + RUN):
-                        values = gate_values(half, gate, tile_index)
-                        if finished is not None:
-                            store_product(*finished)
-                            finished = None
-                        if gate == 0:
-                            input_gates[tile_index] = values
-                        else:
-                            finished = (half, tile_index, input_gates[tile_index], values)
-        store_product(*finished)
+        for index, (half, gate, pair) in enumerate(jobs):
+            values = gate_values(half, gate, pair)
+            if finished is not None:
+                store_products(*finished)
+                finished = None
+            if gate == 0:
+                input_gates[(half, pair)] = values
+            else:
+                finished = (half, pair, input_gates[(half, pair)], values)
+            if index in (2, 4):
+                coming = index // 2 + 1
+                grouped_x = transpose_block(0, coming)
+                grouped_h = transpose_block(1, coming)
+                quantise_block(0, coming, grouped_x)
+                quantise_block(1, coming, grouped_h)
+        store_products(*finished)

@@ -45,7 +45,7 @@ def tile_lstmmirrored_pa_kernel(
     with ExitStack() as ctx:
         keep = ctx.enter_context(tc.tile_pool(name="keep", bufs=1))
         stage = ctx.enter_context(tc.tile_pool(name="stage", bufs=4))
-        gates = ctx.enter_context(tc.tile_pool(name="gates", bufs=6))
+        gates = ctx.enter_context(tc.tile_pool(name="gates", bufs=10))
         psum = ctx.enter_context(tc.psum_pool(name="psum", bufs=8))
         ctx.enter_context(tc.manual_schedule(engines={mybir.EngineType.PE}))
 
@@ -106,11 +106,11 @@ def tile_lstmmirrored_pa_kernel(
         load_activations(1)
         load_scales(0, 1)
         load_codes(0, 0)
-        load_scales(1, 0)
-        load_codes(1, 0)
-        load_scales(1, 1)
         load_activations(2)
         load_activations(3)
+        load_scales(1, 0)
+        load_scales(1, 1)
+        load_codes(1, 0)
         load_codes(0, 1)
         load_codes(1, 1)
 
@@ -207,7 +207,7 @@ def tile_lstmmirrored_pa_kernel(
         quantise_block(0, 1, grouped_x)
         quantise_block(1, 1, grouped_h)
 
-        jobs = [(0, 0, 0), (0, 0, 1), (0, 1, 0), (0, 1, 1), (0, 0, 2), (0, 1, 2), (0, 0, 3), (0, 1, 3)]
+        jobs = [(0, 0, 0), (0, 0, 1), (0, 0, 2), (0, 0, 3), (0, 1, 0), (0, 1, 1), (0, 1, 2), (0, 1, 3)]
         for pair in range(PAIRS):
             for gate in range(2):
                 jobs.append((1, gate, pair))
@@ -223,10 +223,14 @@ def tile_lstmmirrored_pa_kernel(
                 input_gates[(half, pair)] = values
             else:
                 finished = (half, pair, input_gates[(half, pair)], values)
-            if index in (2, 4):
-                coming = index // 2 + 1
-                grouped_x = transpose_block(0, coming)
-                grouped_h = transpose_block(1, coming)
-                quantise_block(0, coming, grouped_x)
-                quantise_block(1, coming, grouped_h)
+            if index == 1:
+                grouped_x = transpose_block(0, 2)
+                grouped_h = transpose_block(1, 2)
+                quantise_block(0, 2, grouped_x)
+                keep_busy(2)
+                quantise_block(1, 2, grouped_h)
+                grouped_x = transpose_block(0, 3)
+                grouped_h = transpose_block(1, 3)
+                quantise_block(0, 3, grouped_x)
+                quantise_block(1, 3, grouped_h)
         store_products(*finished)

@@ -182,9 +182,9 @@ def tile_lstmmirrored_pa_kernel(
                 pair_values.append(values)
             return pair_values
 
-        def store_products(half, pair, input_gates, candidates):
+        def store_products(engine, half, pair, input_gates, candidates):
             for i in range(2):
-                nc.vector.tensor_tensor(out=candidates[i][:], in0=input_gates[i][:], in1=candidates[i][:], op=ALU.mult)
+                engine.tensor_tensor(out=candidates[i][:], in0=input_gates[i][:], in1=candidates[i][:], op=ALU.mult)
                 nc.sync.dma_start(
                     out=out_view[:, 2 * pair + i, BANK * half : BANK * (half + 1)], in_=candidates[i][:]
                 )
@@ -217,7 +217,7 @@ def tile_lstmmirrored_pa_kernel(
         for index, (half, gate, pair) in enumerate(jobs):
             values = gate_values(half, gate, pair)
             if finished is not None:
-                store_products(*finished)
+                store_products(nc.gpsimd, *finished)
                 finished = None
             if gate == 0:
                 input_gates[(half, pair)] = values
@@ -233,4 +233,4 @@ def tile_lstmmirrored_pa_kernel(
                 grouped_h = transpose_block(1, 3)
                 quantise_block(0, 3, grouped_x)
                 quantise_block(1, 3, grouped_h)
-        store_products(*finished)
+        store_products(nc.vector, *finished)

@@ -24,6 +24,7 @@ GROUPS = K_SOURCE // K_PASS
 BANK = 512
 HALVES = N_OUT // BANK
 WORDS = K_PASS // 2
+PIECES = 2
 WARM_UP = 5
 
 FLOPS = 2 * TOKENS * (2 * K_SOURCE) * (2 * N_OUT)
@@ -156,14 +157,14 @@ def tile_lstmmirrored_pa_kernel(
                 copy = nc.scalar.copy if half == 0 else nc.vector.tensor_copy
                 copy(out=bias_all[:, gate, columns], in_=spread[:])
 
-        def gate_values(half, gate, pair):
+        def gate_values(half, gate, pair, members):
             columns = slice(BANK * half, BANK * (half + 1))
-            accs = []
-            for i in range(2):
+            accs = {}
+            for i in members:
                 acc = psum.tile([P, BANK], F32, name="acc", tag="bank")
-                accs.append(acc)
+                accs[i] = acc
             for source in range(2):
-                for i in range(2):
+                for i in members:
                     for g in range(GROUPS):
                         nc.tensor.matmul_mx(
                             out=accs[i][:],
@@ -174,20 +175,46 @@ def tile_lstmmirrored_pa_kernel(
                             start=(source == 0 and g == 0),
                             stop=(source == 1 and g == GROUPS - 1),
                         )
-            pair_values = []
-            for i in range(2):
+            pair_values = {}
+            for i in members:
                 values = gates.tile([P, BANK], F32, name="values_%d" % gate)
                 nc.vector.tensor_tensor(out=values[:], in0=accs[i][:], in1=bias_all[:, gate, columns], op=ALU.add)
                 nc.scalar.activation(out=values[:], in_=values[:], func=gate_function[gate])
-                pair_values.append(values)
+                pair_values[i] = values
             return pair_values
 
-        def store_products(engine, half, pair, input_gates, candidates):
-            for i in range(2):
-                engine.tensor_tensor(out=candidates[i][:], in0=input_gates[i][:], in1=candidates[i][:], op=ALU.mult)
-                nc.sync.dma_start(
-                    out=out_view[:, 2 * pair + i, BANK * half : BANK * (half + 1)], in_=candidates[i][:]
+        def split_candidates(half, pair, i):
+            values = gates.tile([P, BANK], F32, name="values_1")
+            for inner in pieces:
+                columns = slice(BANK * half + inner.start, BANK * half + inner.stop)
+                acc = psum.tile([P, BANK], F32, name="acc", tag="bank")
+                for source in range(2):
+                    for g in range(GROUPS):
+                        nc.tensor.matmul_mx(
+                            out=acc[:, 0 : BANK // PIECES],
+                            lhsT=a_codes[source][pair][:, i, g, :].bitcast(FP8X4),
+                            lhsT_scale=a_planes[source][pair][:, i, g, :],
+                            rhs=w_codes[1][source][half][:, g, inner].bitcast(FP8X4),
+                            rhs_scale=w_planes[1][source][:, g, columns],
+                            start=(source == 0 and g == 0),
+                            stop=(source == 1 and g == GROUPS - 1),
+                        )
+                nc.vector.tensor_tensor(
+                    out=values[:, inner], in0=acc[:, 0 : BANK // PIECES], in1=bias_all[:, 1, columns], op=ALU.add
                 )
+                nc.scalar.activation(out=values[:, inner], in_=values[:, inner], func=gate_function[1])
+            return values
+
+        def store_products(engine, half, pair, input_gates, candidates, spans):
+            for i in sorted(candidates):
+                for inner in spans:
+                    engine.tensor_tensor(
+                        out=candidates[i][:, inner], in0=input_gates[i][:, inner], in1=candidates[i][:, inner], op=ALU.mult
+                    )
+                    nc.sync.dma_start(
+                        out=out_view[:, 2 * pair + i, BANK * half + inner.start : BANK * half + inner.stop],
+                        in_=candidates[i][:, inner],
+                    )
 
         def keep_busy(count):
             idle = psum.tile([P, BANK], F32, name="idle", tag="bank")
@@ -212,25 +239,27 @@ def tile_lstmmirrored_pa_kernel(
             for gate in range(2):
                 jobs.append((1, gate, pair))
 
+        whole = [slice(0, BANK)]
+        pieces = [slice(BANK // PIECES * n, BANK // PIECES * (n + 1)) for n in range(PIECES)]
         input_gates = {}
         finished = None
-        for index, (half, gate, pair) in enumerate(jobs):
-            values = gate_values(half, gate, pair)
+        for index, (half, gate, pair) in enumerate(jobs[:-1]):
+            values = gate_values(half, gate, pair, (0, 1))
             if finished is not None:
-                store_products(nc.gpsimd, *finished)
+                store_products(nc.gpsimd, *finished, whole)
                 finished = None
             if gate == 0:
                 input_gates[(half, pair)] = values
             else:
                 finished = (half, pair, input_gates[(half, pair)], values)
-            if index == 1:
-                grouped_x = transpose_block(0, 2)
-                grouped_h = transpose_block(1, 2)
-                quantise_block(0, 2, grouped_x)
-                keep_busy(2)
-                quantise_block(1, 2, grouped_h)
-                grouped_x = transpose_block(0, 3)
-                grouped_h = transpose_block(1, 3)
-                quantise_block(0, 3, grouped_x)
-                quantise_block(1, 3, grouped_h)
-        store_products(nc.vector, *finished)
+            if index in (0, 1):
+                coming = index + 2
+                grouped_x = transpose_block(0, coming)
+                grouped_h = transpose_block(1, coming)
+                quantise_block(0, coming, grouped_x)
+                quantise_block(1, coming, grouped_h)
+        half, gate, pair = jobs[-1]
+        first = gate_values(half, gate, pair, (0,))
+        second = split_candidates(half, pair, 1)
+        store_products(nc.vector, half, pair, input_gates[(half, pair)], first, whole)
+        store_products(nc.vector, half, pair, input_gates[(half, pair)], {1: second}, pieces)

@@ -86,7 +86,7 @@ def tile_lstmmirrored_pa_kernel(
             scale_words = weight_scales[gate][source].bitcast(I32)
             for r in range(4):
                 nc.sync.dma_start(
-                    out=w_planes[gate][source][r : P : 32, :, :].bitcast(I32),
+                    out=w_planes[gate][source][4 * (2 * gate + source) + r : P : 32, :, :].bitcast(I32),
                     in_=scale_words[:, r : 16 : 4, :].rearrange("g q n -> q g n"),
                 )
 
@@ -171,7 +171,7 @@ def tile_lstmmirrored_pa_kernel(
                             lhsT=a_codes[source][pair][:, i, g, :].bitcast(FP8X4),
                             lhsT_scale=a_planes[source][pair][:, i, g, :],
                             rhs=w_codes[gate][source][half][:, g, :].bitcast(FP8X4),
-                            rhs_scale=w_planes[gate][source][:, g, columns],
+                            rhs_scale=w_planes[gate][source][4 * (2 * gate + source) : P, g, columns],
                             start=(source == 0 and g == 0),
                             stop=(source == 1 and g == GROUPS - 1),
                         )
@@ -195,7 +195,7 @@ def tile_lstmmirrored_pa_kernel(
                             lhsT=a_codes[source][pair][:, i, g, :].bitcast(FP8X4),
                             lhsT_scale=a_planes[source][pair][:, i, g, :],
                             rhs=w_codes[1][source][half][:, g, inner].bitcast(FP8X4),
-                            rhs_scale=w_planes[1][source][:, g, columns],
+                            rhs_scale=w_planes[1][source][4 * (2 + source) : P, g, columns],
                             start=(source == 0 and g == 0),
                             stop=(source == 1 and g == GROUPS - 1),
                         )

@@ -178,9 +178,14 @@ def tile_lstmmirrored_pa_kernel(
             pair_values = {}
             for i in members:
                 values = gates.tile([P, BANK], F32, name="values_%d" % gate)
-                nc.vector.tensor_tensor(out=values[:], in0=accs[i][:], in1=bias_all[:, gate, columns], op=ALU.add)
-                nc.scalar.activation(out=values[:], in_=values[:], func=gate_function[gate])
                 pair_values[i] = values
+                if gate == 0:
+                    nc.scalar.copy(out=values[:], in_=accs[i][:])
+            for i in members:
+                sums = pair_values[i] if gate == 0 else accs[i]
+                nc.vector.tensor_tensor(out=pair_values[i][:], in0=sums[:], in1=bias_all[:, gate, columns], op=ALU.add)
+            for i in members:
+                nc.scalar.activation(out=pair_values[i][:], in_=pair_values[i][:], func=gate_function[gate])
             return pair_values
 
         def split_candidates(half, pair, i):
@@ -246,7 +251,7 @@ def tile_lstmmirrored_pa_kernel(
         for index, (half, gate, pair) in enumerate(jobs[:-1]):
             values = gate_values(half, gate, pair, (0, 1))
             if finished is not None:
-                store_products(nc.gpsimd, *finished, whole)
+                store_products(nc.vector, *finished, whole)
                 finished = None
             if gate == 0:
                 input_gates[(half, pair)] = values

@@ -24,6 +24,10 @@ GROUPS = K_SOURCE // K_PASS
 BANK = 512
 HALVES = N_OUT // BANK
 WORDS = K_PASS // 2
+SQ = 32
+QK = 128
+BLOCKS = 2 * P // SQ
+WORDS_PAIR = GROUPS * BLOCKS * QK // 2
 PIECES = 2
 WARM_UP = 5
 
@@ -40,15 +44,22 @@ def tile_lstmmirrored_pa_kernel(
     biases = (b_i, b_c)
     gate_function = (ACT.Sigmoid, ACT.Tanh)
 
-    source_view = [a.rearrange("(p t) k -> p t k", t=TILES) for a in (x, hist)]
-    out_view = out.rearrange("(p t) n -> p t n", t=TILES)
+    half_tokens = TOKENS // 2
+    half_tiles = TILES // 2
+    source_view = [a[0:half_tokens, :].rearrange("(p t) k -> p t k", t=half_tiles) for a in (x, hist)]
+    out_view = out[0:half_tokens, :].rearrange("(p t) n -> p t n", t=half_tiles)
+
+    def out_rows(tile):
+        if tile < half_tiles:
+            return out_view[:, tile, :]
+        return out[P * tile : P * (tile + 1), :]
 
     with ExitStack() as ctx:
         keep = ctx.enter_context(tc.tile_pool(name="keep", bufs=1))
         stage = ctx.enter_context(tc.tile_pool(name="stage", bufs=4))
         gates = ctx.enter_context(tc.tile_pool(name="gates", bufs=10))
         psum = ctx.enter_context(tc.psum_pool(name="psum", bufs=8))
-        ctx.enter_context(tc.manual_schedule(engines={mybir.EngineType.PE}))
+        ctx.enter_context(tc.manual_schedule(engines={mybir.EngineType.PE, mybir.EngineType.Activation, mybir.EngineType.DVE}))
 
         ones = keep.tile([P, BANK], BF16, name="ones")
         nc.vector.memset(ones[:], 1.0)
@@ -73,6 +84,7 @@ def tile_lstmmirrored_pa_kernel(
 
 
         raw = [[None] * PAIRS for source in range(2)]
+        blocked = [[None] * PAIRS for source in range(2)]
         w_codes = [[[None] * HALVES for source in range(2)] for gate in range(2)]
 
         def load_activations(pair):
@@ -81,6 +93,21 @@ def tile_lstmmirrored_pa_kernel(
                 nc.sync.dma_start(
                     out=raw[source][pair][:], in_=source_view[source][:, 2 * pair : 2 * pair + 2, :]
                 )
+
+        def load_blocked(pair):
+            first = 2 * P * pair
+            for source in range(2):
+                tile_in = keep.tile([P, GROUPS, BLOCKS, QK], BF16, name="blocked_%d_%d" % (source, pair), align_bytes=64)
+                blocked[source][pair] = tile_in
+                for g in range(GROUPS):
+                    for q in range(4):
+                        begin = K_PASS * g + QK * q
+                        nc.sync.dma_start(
+                            out=tile_in[SQ * q : SQ * (q + 1), g, :, :],
+                            in_=(x, hist)[source][first : first + 2 * P, begin : begin + QK].rearrange(
+                                "(b j) k -> j b k", j=SQ
+                            ),
+                        )
 
         def load_scales(gate, source):
             scale_words = weight_scales[gate][source].bitcast(I32)
@@ -107,19 +134,19 @@ def tile_lstmmirrored_pa_kernel(
         load_activations(1)
         load_scales(0, 1)
         load_codes(0, 0)
-        load_activations(2)
-        load_activations(3)
         load_scales(1, 0)
         load_scales(1, 1)
         load_codes(1, 0)
         load_codes(0, 1)
+        load_blocked(2)
         load_codes(1, 1)
+        load_blocked(3)
 
         a_codes = [[None] * PAIRS for source in range(2)]
         a_planes = [[None] * PAIRS for source in range(2)]
 
         def transpose_block(source, pair):
-            grouped = stage.tile([P, 2, GROUPS, P, PACK], BF16, name="grouped", align_bytes=64)
+            grouped = stage.tile([P, GROUPS, 2, P, PACK], BF16, name="grouped", align_bytes=64)
             for i in range(2):
                 words = raw[source][pair][:, i, :].bitcast(F32)
                 flipped = psum.tile([P, GROUPS, 2, P], F32, name="flipped", tag="bank")
@@ -129,20 +156,45 @@ def tile_lstmmirrored_pa_kernel(
                             flipped[:, g, u, :], words[:, WORDS * g + u : WORDS * (g + 1) : 2], identity[:]
                         )
                 copy = nc.scalar.copy if i == 0 else nc.vector.tensor_copy
-                copy(out=grouped[:, i].bitcast(F32), in_=flipped[:].rearrange("p g u r -> p g r u"))
+                copy(out=grouped[:, :, i].bitcast(F32), in_=flipped[:].rearrange("p g u r -> p g r u"))
+            return grouped
+
+        def order_words(source, pair):
+            ordered = stage.tile([P, WORDS_PAIR], F32, name="ordered", align_bytes=64)
+            nc.scalar.copy(
+                out=ordered[:].rearrange("p (a u w) -> p a u w", u=2, w=SQ),
+                in_=blocked[source][pair][:].rearrange("p g b k -> p (g b k)").bitcast(F32).rearrange(
+                    "p (a w u) -> p a u w", u=2, w=SQ
+                ),
+            )
+            return ordered
+
+        def turn(ordered):
+            turned = stage.tile([P, WORDS_PAIR], F32, name="turned", align_bytes=64)
+            nc.vector.transpose(out=turned[:], in_=ordered[:])
+            return turned
+
+        def interleave(turned):
+            grouped = stage.tile([P, GROUPS, 2, P, PACK], BF16, name="grouped", align_bytes=64)
+            nc.vector.tensor_copy(
+                out=grouped[:].rearrange("p g i r t -> p (g i r t)").bitcast(F32).rearrange(
+                    "p (a j u) -> p a j u", u=2, j=SQ
+                ),
+                in_=turned[:].rearrange("p (a u j) -> p a j u", u=2, j=SQ),
+            )
             return grouped
 
         def quantise_block(source, pair, grouped):
             a_codes[source][pair] = keep.tile(
-                [P, 2, GROUPS, P], U32, name="a_codes_%d_%d" % (source, pair), align_bytes=64
+                [P, GROUPS, 2, P], U32, name="a_codes_%d_%d" % (source, pair), align_bytes=64
             )
             a_planes[source][pair] = keep.tile(
-                [P, 2, GROUPS, P], U8, name="a_planes_%d_%d" % (source, pair), align_bytes=64
+                [P, GROUPS, 2, P], U8, name="a_planes_%d_%d" % (source, pair), align_bytes=64
             )
             nc.vector.quantize_mx(
-                out=a_codes[source][pair][:].rearrange("p i g r -> p (i g r)").bitcast(FP8X4),
-                scales=a_planes[source][pair][:].rearrange("p i g r -> p (i g r)"),
-                in_=grouped[:].rearrange("p i g r t -> p (i g r t)"),
+                out=a_codes[source][pair][:].rearrange("p g i r -> p (g i r)").bitcast(FP8X4),
+                scales=a_planes[source][pair][:].rearrange("p g i r -> p (g i r)"),
+                in_=grouped[:].rearrange("p g i r t -> p (g i r t)"),
             )
 
         bias_all = keep.tile([P, 2, N_OUT], F32, name="bias_all")
@@ -168,8 +220,8 @@ def tile_lstmmirrored_pa_kernel(
                     for g in range(GROUPS):
                         nc.tensor.matmul_mx(
                             out=accs[i][:],
-                            lhsT=a_codes[source][pair][:, i, g, :].bitcast(FP8X4),
-                            lhsT_scale=a_planes[source][pair][:, i, g, :],
+                            lhsT=a_codes[source][pair][:, g, i, :].bitcast(FP8X4),
+                            lhsT_scale=a_planes[source][pair][:, g, i, :],
                             rhs=w_codes[gate][source][half][:, g, :].bitcast(FP8X4),
                             rhs_scale=w_planes[gate][source][4 * (2 * gate + source) : P, g, columns],
                             start=(source == 0 and g == 0),
@@ -179,11 +231,8 @@ def tile_lstmmirrored_pa_kernel(
             for i in members:
                 values = gates.tile([P, BANK], F32, name="values_%d" % gate)
                 pair_values[i] = values
-                if gate == 0:
-                    nc.scalar.copy(out=values[:], in_=accs[i][:])
             for i in members:
-                sums = pair_values[i] if gate == 0 else accs[i]
-                nc.vector.tensor_tensor(out=pair_values[i][:], in0=sums[:], in1=bias_all[:, gate, columns], op=ALU.add)
+                nc.vector.tensor_tensor(out=pair_values[i][:], in0=accs[i][:], in1=bias_all[:, gate, columns], op=ALU.add)
             for i in members:
                 nc.scalar.activation(out=pair_values[i][:], in_=pair_values[i][:], func=gate_function[gate])
             return pair_values
@@ -197,8 +246,8 @@ def tile_lstmmirrored_pa_kernel(
                     for g in range(GROUPS):
                         nc.tensor.matmul_mx(
                             out=acc[:, 0 : BANK // PIECES],
-                            lhsT=a_codes[source][pair][:, i, g, :].bitcast(FP8X4),
-                            lhsT_scale=a_planes[source][pair][:, i, g, :],
+                            lhsT=a_codes[source][pair][:, g, i, :].bitcast(FP8X4),
+                            lhsT_scale=a_planes[source][pair][:, g, i, :],
                             rhs=w_codes[1][source][half][:, g, inner].bitcast(FP8X4),
                             rhs_scale=w_planes[1][source][4 * (2 + source) : P, g, columns],
                             start=(source == 0 and g == 0),
@@ -217,7 +266,7 @@ def tile_lstmmirrored_pa_kernel(
                         out=candidates[i][:, inner], in0=input_gates[i][:, inner], in1=candidates[i][:, inner], op=ALU.mult
                     )
                     nc.sync.dma_start(
-                        out=out_view[:, 2 * pair + i, BANK * half + inner.start : BANK * half + inner.stop],
+                        out=out_rows(2 * pair + i)[:, BANK * half + inner.start : BANK * half + inner.stop],
                         in_=candidates[i][:, inner],
                     )
 
@@ -239,30 +288,36 @@ def tile_lstmmirrored_pa_kernel(
         quantise_block(0, 1, grouped_x)
         quantise_block(1, 1, grouped_h)
 
-        jobs = [(0, 0, 0), (0, 0, 1), (0, 0, 2), (0, 0, 3), (0, 1, 0), (0, 1, 1), (0, 1, 2), (0, 1, 3)]
-        for pair in range(PAIRS):
+        jobs = []
+        for half in range(HALVES):
             for gate in range(2):
-                jobs.append((1, gate, pair))
+                for pair in (0, 1):
+                    jobs.append((half, gate, pair))
+        for pair in (2, 3):
+            for half in range(HALVES):
+                for gate in range(2):
+                    jobs.append((half, gate, pair))
 
         whole = [slice(0, BANK)]
         pieces = [slice(BANK // PIECES * n, BANK // PIECES * (n + 1)) for n in range(PIECES)]
         input_gates = {}
+        ordered = {}
         finished = None
         for index, (half, gate, pair) in enumerate(jobs[:-1]):
             values = gate_values(half, gate, pair, (0, 1))
             if finished is not None:
-                store_products(nc.vector, *finished, whole)
+                store_products(nc.gpsimd, *finished, whole)
                 finished = None
             if gate == 0:
                 input_gates[(half, pair)] = values
             else:
                 finished = (half, pair, input_gates[(half, pair)], values)
-            if index in (0, 1):
-                coming = index + 2
-                grouped_x = transpose_block(0, coming)
-                grouped_h = transpose_block(1, coming)
-                quantise_block(0, coming, grouped_x)
-                quantise_block(1, coming, grouped_h)
+            for source in range(2):
+                for coming, begin in ((2, 3), (3, 6)):
+                    if index == begin + source:
+                        ordered[source] = order_words(source, coming)
+                    if index == begin + source + 1:
+                        quantise_block(source, coming, interleave(turn(ordered[source])))
         half, gate, pair = jobs[-1]
         first = gate_values(half, gate, pair, (0,))
         second = split_candidates(half, pair, 1)

@@ -28,6 +28,7 @@ SQ = 32
 QK = 128
 BLOCKS = 2 * P // SQ
 WORDS_PAIR = GROUPS * BLOCKS * QK // 2
+TENSOR_TILES = 6
 PIECES = 2
 WARM_UP = 5
 
@@ -44,13 +45,12 @@ def tile_lstmmirrored_pa_kernel(
     biases = (b_i, b_c)
     gate_function = (ACT.Sigmoid, ACT.Tanh)
 
-    half_tokens = TOKENS // 2
-    half_tiles = TILES // 2
-    source_view = [a[0:half_tokens, :].rearrange("(p t) k -> p t k", t=half_tiles) for a in (x, hist)]
-    out_view = out[0:half_tokens, :].rearrange("(p t) n -> p t n", t=half_tiles)
+    tensor_tokens = TENSOR_TILES * P
+    source_view = [a[0:tensor_tokens, :].rearrange("(p t) k -> p t k", t=TENSOR_TILES) for a in (x, hist)]
+    out_view = out[0:tensor_tokens, :].rearrange("(p t) n -> p t n", t=TENSOR_TILES)
 
     def out_rows(tile):
-        if tile < half_tiles:
+        if tile < TENSOR_TILES:
             return out_view[:, tile, :]
         return out[P * tile : P * (tile + 1), :]
 
@@ -134,11 +134,11 @@ def tile_lstmmirrored_pa_kernel(
         load_activations(1)
         load_scales(0, 1)
         load_codes(0, 0)
+        load_activations(2)
         load_scales(1, 0)
         load_scales(1, 1)
         load_codes(1, 0)
         load_codes(0, 1)
-        load_blocked(2)
         load_codes(1, 1)
         load_blocked(3)
 
@@ -291,9 +291,9 @@ def tile_lstmmirrored_pa_kernel(
         jobs = []
         for half in range(HALVES):
             for gate in range(2):
-                for pair in (0, 1):
+                for pair in (0, 1, 2):
                     jobs.append((half, gate, pair))
-        for pair in (2, 3):
+        for pair in (3,):
             for half in range(HALVES):
                 for gate in range(2):
                     jobs.append((half, gate, pair))
@@ -306,14 +306,19 @@ def tile_lstmmirrored_pa_kernel(
         for index, (half, gate, pair) in enumerate(jobs[:-1]):
             values = gate_values(half, gate, pair, (0, 1))
             if finished is not None:
-                store_products(nc.gpsimd, *finished, whole)
+                store_products(nc.gpsimd if 10 <= index <= 12 else nc.vector, *finished, whole)
                 finished = None
             if gate == 0:
                 input_gates[(half, pair)] = values
             else:
                 finished = (half, pair, input_gates[(half, pair)], values)
+            if index == 0:
+                grouped_x = transpose_block(0, 2)
+                grouped_h = transpose_block(1, 2)
+                quantise_block(0, 2, grouped_x)
+                quantise_block(1, 2, grouped_h)
             for source in range(2):
-                for coming, begin in ((2, 3), (3, 6)):
+                for coming, begin in ((3, 6),):
                     if index == begin + source:
                         ordered[source] = order_words(source, coming)
                     if index == begin + source + 1:

@@ -139,8 +139,8 @@ def tile_lstmmirrored_pa_kernel(
         load_scales(1, 1)
         load_codes(1, 0)
         load_codes(0, 1)
-        load_codes(1, 1)
         load_blocked(3)
+        load_codes(1, 1)
 
         a_codes = [[None] * PAIRS for source in range(2)]
         a_planes = [[None] * PAIRS for source in range(2)]
@@ -306,7 +306,7 @@ def tile_lstmmirrored_pa_kernel(
         for index, (half, gate, pair) in enumerate(jobs[:-1]):
             values = gate_values(half, gate, pair, (0, 1))
             if finished is not None:
-                store_products(nc.gpsimd if 10 <= index <= 12 else nc.vector, *finished, whole)
+                store_products(nc.gpsimd if index in (4, 5, 10, 11, 12) else nc.vector, *finished, whole)
                 finished = None
             if gate == 0:
                 input_gates[(half, pair)] = values
@@ -318,7 +318,7 @@ def tile_lstmmirrored_pa_kernel(
                 quantise_block(0, 2, grouped_x)
                 quantise_block(1, 2, grouped_h)
             for source in range(2):
-                for coming, begin in ((3, 6),):
+                for coming, begin in ((3, 5),):
                     if index == begin + source:
                         ordered[source] = order_words(source, coming)
                     if index == begin + source + 1:

@@ -57,7 +57,7 @@ def tile_lstmmirrored_pa_kernel(
     with ExitStack() as ctx:
         keep = ctx.enter_context(tc.tile_pool(name="keep", bufs=1))
         stage = ctx.enter_context(tc.tile_pool(name="stage", bufs=4))
-        gates = ctx.enter_context(tc.tile_pool(name="gates", bufs=10))
+        gates = ctx.enter_context(tc.tile_pool(name="gates", bufs=14))
         psum = ctx.enter_context(tc.psum_pool(name="psum", bufs=8))
         ctx.enter_context(tc.manual_schedule(engines={mybir.EngineType.PE, mybir.EngineType.Activation, mybir.EngineType.DVE}))
 
@@ -94,20 +94,19 @@ def tile_lstmmirrored_pa_kernel(
                     out=raw[source][pair][:], in_=source_view[source][:, 2 * pair : 2 * pair + 2, :]
                 )
 
-        def load_blocked(pair):
+        def load_blocked(pair, source):
             first = 2 * P * pair
-            for source in range(2):
-                tile_in = keep.tile([P, GROUPS, BLOCKS, QK], BF16, name="blocked_%d_%d" % (source, pair), align_bytes=64)
-                blocked[source][pair] = tile_in
-                for g in range(GROUPS):
-                    for q in range(4):
-                        begin = K_PASS * g + QK * q
-                        nc.sync.dma_start(
-                            out=tile_in[SQ * q : SQ * (q + 1), g, :, :],
-                            in_=(x, hist)[source][first : first + 2 * P, begin : begin + QK].rearrange(
-                                "(b j) k -> j b k", j=SQ
-                            ),
-                        )
+            tile_in = keep.tile([P, GROUPS, BLOCKS, QK], BF16, name="blocked_%d_%d" % (source, pair), align_bytes=64)
+            blocked[source][pair] = tile_in
+            for g in range(GROUPS):
+                for q in range(4):
+                    begin = K_PASS * g + QK * q
+                    nc.sync.dma_start(
+                        out=tile_in[SQ * q : SQ * (q + 1), g, :, :],
+                        in_=(x, hist)[source][first : first + 2 * P, begin : begin + QK].rearrange(
+                            "(b j) k -> j b k", j=SQ
+                        ),
+                    )
 
         def load_scales(gate, source):
             scale_words = weight_scales[gate][source].bitcast(I32)
@@ -135,11 +134,12 @@ def tile_lstmmirrored_pa_kernel(
         load_scales(0, 1)
         load_codes(0, 0)
         load_activations(2)
+        load_codes(0, 1)
+        load_blocked(3, 0)
         load_scales(1, 0)
         load_scales(1, 1)
         load_codes(1, 0)
-        load_codes(0, 1)
-        load_blocked(3)
+        load_blocked(3, 1)
         load_codes(1, 1)
 
         a_codes = [[None] * PAIRS for source in range(2)]
@@ -289,14 +289,13 @@ def tile_lstmmirrored_pa_kernel(
         quantise_block(1, 1, grouped_h)
 
         jobs = []
-        for half in range(HALVES):
-            for gate in range(2):
+        for gate in range(2):
+            for half in range(HALVES):
                 for pair in (0, 1, 2):
                     jobs.append((half, gate, pair))
-        for pair in (3,):
-            for half in range(HALVES):
-                for gate in range(2):
-                    jobs.append((half, gate, pair))
+        for half in range(HALVES):
+            for gate in range(2):
+                jobs.append((half, gate, 3))
 
         whole = [slice(0, BANK)]
         pieces = [slice(BANK // PIECES * n, BANK // PIECES * (n + 1)) for n in range(PIECES)]
@@ -306,7 +305,7 @@ def tile_lstmmirrored_pa_kernel(
         for index, (half, gate, pair) in enumerate(jobs[:-1]):
             values = gate_values(half, gate, pair, (0, 1))
             if finished is not None:
-                store_products(nc.gpsimd if index in (4, 5, 10, 11, 12) else nc.vector, *finished, whole)
+                store_products(nc.gpsimd if 9 <= index <= 12 else nc.vector, *finished, whole)
                 finished = None
             if gate == 0:
                 input_gates[(half, pair)] = values
@@ -318,11 +317,10 @@ def tile_lstmmirrored_pa_kernel(
                 quantise_block(0, 2, grouped_x)
                 quantise_block(1, 2, grouped_h)
             for source in range(2):
-                for coming, begin in ((3, 5),):
-                    if index == begin + source:
-                        ordered[source] = order_words(source, coming)
-                    if index == begin + source + 1:
-                        quantise_block(source, coming, interleave(turn(ordered[source])))
+                if index == (3, 6)[source]:
+                    ordered[source] = order_words(source, 3)
+                if index == (4, 7)[source]:
+                    quantise_block(source, 3, interleave(turn(ordered[source])))
         half, gate, pair = jobs[-1]
         first = gate_values(half, gate, pair, (0,))
         second = split_candidates(half, pair, 1)

@@ -29,7 +29,6 @@ QK = 128
 BLOCKS = 2 * P // SQ
 WORDS_PAIR = GROUPS * BLOCKS * QK // 2
 TENSOR_TILES = 6
-PIECES = 2
 WARM_UP = 5
 
 FLOPS = 2 * TOKENS * (2 * K_SOURCE) * (2 * N_OUT)
@@ -176,7 +175,7 @@ def tile_lstmmirrored_pa_kernel(
 
         def interleave(turned):
             grouped = stage.tile([P, GROUPS, 2, P, PACK], BF16, name="grouped", align_bytes=64)
-            nc.vector.tensor_copy(
+            nc.scalar.copy(
                 out=grouped[:].rearrange("p g i r t -> p (g i r t)").bitcast(F32).rearrange(
                     "p (a j u) -> p a j u", u=2, j=SQ
                 ),
@@ -209,13 +208,15 @@ def tile_lstmmirrored_pa_kernel(
                 copy = nc.scalar.copy if half == 0 else nc.vector.tensor_copy
                 copy(out=bias_all[:, gate, columns], in_=spread[:])
 
-        def gate_values(half, gate, pair, members):
+        def gate_values(half, gate, pair, members, between_sources=None):
             columns = slice(BANK * half, BANK * (half + 1))
             accs = {}
             for i in members:
                 acc = psum.tile([P, BANK], F32, name="acc", tag="bank")
                 accs[i] = acc
             for source in range(2):
+                if source == 1 and between_sources is not None:
+                    between_sources()
                 for i in members:
                     for g in range(GROUPS):
                         nc.tensor.matmul_mx(
@@ -245,7 +246,7 @@ def tile_lstmmirrored_pa_kernel(
                 for source in range(2):
                     for g in range(GROUPS):
                         nc.tensor.matmul_mx(
-                            out=acc[:, 0 : BANK // PIECES],
+                            out=acc[:, 0 : inner.stop - inner.start],
                             lhsT=a_codes[source][pair][:, g, i, :].bitcast(FP8X4),
                             lhsT_scale=a_planes[source][pair][:, g, i, :],
                             rhs=w_codes[1][source][half][:, g, inner].bitcast(FP8X4),
@@ -254,7 +255,7 @@ def tile_lstmmirrored_pa_kernel(
                             stop=(source == 1 and g == GROUPS - 1),
                         )
                 nc.vector.tensor_tensor(
-                    out=values[:, inner], in0=acc[:, 0 : BANK // PIECES], in1=bias_all[:, 1, columns], op=ALU.add
+                    out=values[:, inner], in0=acc[:, 0 : inner.stop - inner.start], in1=bias_all[:, 1, columns], op=ALU.add
                 )
                 nc.scalar.activation(out=values[:, inner], in_=values[:, inner], func=gate_function[1])
             return values
@@ -293,36 +294,43 @@ def tile_lstmmirrored_pa_kernel(
             for half in range(HALVES):
                 for pair in (0, 1, 2):
                     jobs.append((half, gate, pair))
-        for half in range(HALVES):
-            for gate in range(2):
-                jobs.append((half, gate, 3))
+        for gate in range(2):
+            jobs.append((0, gate, 3))
 
         whole = [slice(0, BANK)]
-        pieces = [slice(BANK // PIECES * n, BANK // PIECES * (n + 1)) for n in range(PIECES)]
+        pieces = [slice(0, BANK // 2), slice(BANK // 2, 3 * BANK // 4), slice(3 * BANK // 4, BANK)]
         input_gates = {}
-        ordered = {}
+        steps = {}
         finished = None
-        for index, (half, gate, pair) in enumerate(jobs[:-1]):
-            values = gate_values(half, gate, pair, (0, 1))
+
+        def third_hist():
+            quantise_block(1, 2, transpose_block(1, 2))
+
+        for index, (half, gate, pair) in enumerate(jobs):
+            values = gate_values(half, gate, pair, (0, 1), third_hist if index == 1 else None)
             if finished is not None:
-                store_products(nc.gpsimd if 9 <= index <= 12 else nc.vector, *finished, whole)
+                store_products(nc.gpsimd if index in (9, 11, 12) else nc.vector, *finished, whole)
                 finished = None
             if gate == 0:
                 input_gates[(half, pair)] = values
             else:
                 finished = (half, pair, input_gates[(half, pair)], values)
             if index == 0:
-                grouped_x = transpose_block(0, 2)
-                grouped_h = transpose_block(1, 2)
-                quantise_block(0, 2, grouped_x)
-                quantise_block(1, 2, grouped_h)
-            for source in range(2):
-                if index == (3, 6)[source]:
-                    ordered[source] = order_words(source, 3)
-                if index == (4, 7)[source]:
-                    quantise_block(source, 3, interleave(turn(ordered[source])))
-        half, gate, pair = jobs[-1]
-        first = gate_values(half, gate, pair, (0,))
+                quantise_block(0, 2, transpose_block(0, 2))
+            for source, begin in enumerate((3, 6)):
+                if index == begin:
+                    steps[source] = order_words(source, 3)
+                if index == begin + 1:
+                    steps[source] = interleave(turn(steps[source]))
+                if index == begin + 2:
+                    quantise_block(source, 3, steps[source])
+        half, pair = HALVES - 1, PAIRS - 1
+        first_gates = gate_values(half, 0, pair, (0,))
+        products_half, products_pair, products_gates, candidates = finished
+        for engine, i in ((nc.gpsimd, 0), (nc.vector, 1)):
+            store_products(engine, products_half, products_pair, products_gates, {i: candidates[i]}, whole)
+        first = gate_values(half, 1, pair, (0,))
+        second_gates = gate_values(half, 0, pair, (1,))
+        store_products(nc.gpsimd, half, pair, first_gates, first, whole)
         second = split_candidates(half, pair, 1)
-        store_products(nc.vector, half, pair, input_gates[(half, pair)], first, whole)
-        store_products(nc.vector, half, pair, input_gates[(half, pair)], {1: second}, pieces)
+        store_products(nc.vector, half, pair, second_gates, {1: second}, pieces)

@@ -60,26 +60,23 @@ def tile_lstmmirrored_pa_kernel(
         psum = ctx.enter_context(tc.psum_pool(name="psum", bufs=8))
         ctx.enter_context(tc.manual_schedule(engines={mybir.EngineType.PE, mybir.EngineType.Activation, mybir.EngineType.DVE}))
 
+        bias_rows = keep.tile([P, 2, N_OUT], BF16, name="bias_rows")
+        nc.gpsimd.memset(bias_rows[:].rearrange("p a n -> p (a n)").bitcast(I32), 0)
+        identity = keep.tile([P, P], F32, name="identity")
+        masks.make_identity(nc, identity[:])
+
         ones = keep.tile([P, BANK], BF16, name="ones")
         nc.vector.memset(ones[:], 1.0)
-        bias_rows = keep.tile([P, 2, N_OUT], BF16, name="bias_rows")
-        nc.vector.memset(bias_rows[:].rearrange("p a n -> p (a n)").bitcast(I32), 0)
-        for gate in range(2):
-            nc.scalar.dma_start(out=bias_rows[0:1, gate, :], in_=biases[gate].unsqueeze(0))
-
         warm = keep.tile([P, 1], F32, name="warm")
         nc.vector.memset(warm[:], 0.0)
         nc.scalar.activation(out=warm[:], in_=warm[:], func=ACT.Sigmoid)
 
         w_planes = [[None] * 2 for gate in range(2)]
-        for gate in range(2):
+        for gate, engine in ((0, nc.vector), (1, nc.gpsimd)):
             for source in range(2):
                 planes = keep.tile([P, GROUPS, N_OUT], U8, name="w_planes_%d_%d" % (gate, source), align_bytes=64)
-                nc.vector.memset(planes[:].rearrange("p g n -> p (g n)").bitcast(I32), 0)
+                engine.memset(planes[:].rearrange("p g n -> p (g n)").bitcast(I32), 0)
                 w_planes[gate][source] = planes
-
-        identity = keep.tile([P, P], F32, name="identity")
-        masks.make_identity(nc, identity[:])
 
 
         raw = [[None] * PAIRS for source in range(2)]
@@ -115,8 +112,8 @@ def tile_lstmmirrored_pa_kernel(
                     in_=scale_words[:, r : 16 : 4, :].rearrange("g q n -> q g n"),
                 )
 
-        def load_codes(gate, half):
-            for source in range(2):
+        def load_codes(gate, half, sources=(0, 1)):
+            for source in sources:
                 codes = keep.tile(
                     [P, GROUPS, BANK], U32, name="w_codes_%d_%d_%d" % (gate, source, half), align_bytes=64
                 )
@@ -128,10 +125,12 @@ def tile_lstmmirrored_pa_kernel(
                 w_codes[gate][source][half] = codes
 
         load_activations(0)
-        load_scales(0, 0)
+        for gate in range(2):
+            nc.sync.dma_start(out=bias_rows[0:1, gate, :], in_=biases[gate].unsqueeze(0))
         load_activations(1)
-        load_scales(0, 1)
-        load_codes(0, 0)
+        for source in range(2):
+            load_scales(0, source)
+            load_codes(0, 0, (source,))
         load_activations(2)
         load_codes(0, 1)
         load_blocked(3, 0)
@@ -289,11 +288,10 @@ def tile_lstmmirrored_pa_kernel(
         quantise_block(0, 1, grouped_x)
         quantise_block(1, 1, grouped_h)
 
-        jobs = []
-        for gate in range(2):
-            for half in range(HALVES):
-                for pair in (0, 1, 2):
-                    jobs.append((half, gate, pair))
+        jobs = [(0, 0, 0), (0, 0, 1), (1, 0, 0), (0, 0, 2), (1, 0, 1), (1, 0, 2)]
+        for half in range(HALVES):
+            for pair in (0, 1, 2):
+                jobs.append((half, 1, pair))
         for gate in range(2):
             jobs.append((0, gate, 3))
 
@@ -303,11 +301,11 @@ def tile_lstmmirrored_pa_kernel(
         steps = {}
         finished = None
 
-        def third_hist():
-            quantise_block(1, 2, transpose_block(1, 2))
+        def third_x():
+            quantise_block(0, 2, transpose_block(0, 2))
 
         for index, (half, gate, pair) in enumerate(jobs):
-            values = gate_values(half, gate, pair, (0, 1), third_hist if index == 1 else None)
+            values = gate_values(half, gate, pair, (0, 1), third_x if index == 1 else None)
             if finished is not None:
                 store_products(nc.gpsimd if index in (9, 11, 12) else nc.vector, *finished, whole)
                 finished = None
@@ -315,8 +313,8 @@ def tile_lstmmirrored_pa_kernel(
                 input_gates[(half, pair)] = values
             else:
                 finished = (half, pair, input_gates[(half, pair)], values)
-            if index == 0:
-                quantise_block(0, 2, transpose_block(0, 2))
+            if index == 1:
+                quantise_block(1, 2, transpose_block(1, 2))
             for source, begin in enumerate((3, 6)):
                 if index == begin:
                     steps[source] = order_words(source, 3)
@@ -331,6 +329,6 @@ def tile_lstmmirrored_pa_kernel(
             store_products(engine, products_half, products_pair, products_gates, {i: candidates[i]}, whole)
         first = gate_values(half, 1, pair, (0,))
         second_gates = gate_values(half, 0, pair, (1,))
-        store_products(nc.gpsimd, half, pair, first_gates, first, whole)
         second = split_candidates(half, pair, 1)
+        store_products(nc.vector, half, pair, first_gates, first, whole)
         store_products(nc.vector, half, pair, second_gates, {1: second}, pieces)

from contextlib import ExitStack

import concourse.masks as masks
import concourse.mybir as mybir

F32 = mybir.dt.float32
BF16 = mybir.dt.bfloat16
I32 = mybir.dt.int32
U32 = mybir.dt.uint32
U8 = mybir.dt.uint8
FP8X4 = mybir.dt.float8_e4m3fn_x4
ACT = mybir.ActivationFunctionType
ALU = mybir.AluOpType

P = 128
PACK = 4
K_PASS = P * PACK
TOKENS = 1024
K_SOURCE = 1024
N_OUT = 1024
TILES = TOKENS // P
PAIRS = TILES // 2
GROUPS = K_SOURCE // K_PASS
BANK = 512
HALVES = N_OUT // BANK
WORDS = K_PASS // 2
SQ = 32
QK = 128
BLOCKS = 2 * P // SQ
WORDS_PAIR = GROUPS * BLOCKS * QK // 2
TENSOR_TILES = 6
WARM_UP = 5

FLOPS = 2 * TOKENS * (2 * K_SOURCE) * (2 * N_OUT)


def tile_lstmmirrored_pa_kernel(
    tc, x, hist, Wix_words, Wix_scales, Wih_words, Wih_scales, b_i,
    Wcx_words, Wcx_scales, Wch_words, Wch_scales, b_c, out,
):
    nc = tc.nc
    weight_words = ((Wix_words, Wih_words), (Wcx_words, Wch_words))
    weight_scales = ((Wix_scales, Wih_scales), (Wcx_scales, Wch_scales))
    biases = (b_i, b_c)
    gate_function = (ACT.Sigmoid, ACT.Tanh)

    tensor_tokens = TENSOR_TILES * P
    source_view = [a[0:tensor_tokens, :].rearrange("(p t) k -> p t k", t=TENSOR_TILES) for a in (x, hist)]
    out_view = out[0:tensor_tokens, :].rearrange("(p t) n -> p t n", t=TENSOR_TILES)

    def out_rows(tile):
        if tile < TENSOR_TILES:
            return out_view[:, tile, :]
        return out[P * tile : P * (tile + 1), :]

    with ExitStack() as ctx:
        keep = ctx.enter_context(tc.tile_pool(name="keep", bufs=1))
        stage = ctx.enter_context(tc.tile_pool(name="stage", bufs=4))
        gates = ctx.enter_context(tc.tile_pool(name="gates", bufs=14))
        psum = ctx.enter_context(tc.psum_pool(name="psum", bufs=8))
        ctx.enter_context(tc.manual_schedule(engines={mybir.EngineType.PE, mybir.EngineType.Activation, mybir.EngineType.DVE}))

        bias_rows = keep.tile([P, 2, N_OUT], BF16, name="bias_rows")
        nc.gpsimd.memset(bias_rows[:].rearrange("p a n -> p (a n)").bitcast(I32), 0)
        identity = keep.tile([P, P], F32, name="identity")
        masks.make_identity(nc, identity[:])

        ones = keep.tile([P, BANK], BF16, name="ones")
        nc.vector.memset(ones[:], 1.0)
        warm = keep.tile([P, 1], F32, name="warm")
        nc.vector.memset(warm[:], 0.0)
        nc.scalar.activation(out=warm[:], in_=warm[:], func=ACT.Sigmoid)

        w_planes = [[None] * 2 for gate in range(2)]
        for gate, engine in ((0, nc.vector), (1, nc.gpsimd)):
            for source in range(2):
                planes = keep.tile([P, GROUPS, N_OUT], U8, name="w_planes_%d_%d" % (gate, source), align_bytes=64)
                engine.memset(planes[:].rearrange("p g n -> p (g n)").bitcast(I32), 0)
                w_planes[gate][source] = planes


        raw = [[None] * PAIRS for source in range(2)]
        blocked = [[None] * PAIRS for source in range(2)]
        w_codes = [[[None] * HALVES for source in range(2)] for gate in range(2)]

        def load_activations(pair):
            for source in range(2):
                raw[source][pair] = keep.tile([P, 2, K_SOURCE], BF16, name="raw_%d_%d" % (source, pair))
                nc.sync.dma_start(
                    out=raw[source][pair][:], in_=source_view[source][:, 2 * pair : 2 * pair + 2, :]
                )

        def load_blocked(pair, source):
            first = 2 * P * pair
            tile_in = keep.tile([P, GROUPS, BLOCKS, QK], BF16, name="blocked_%d_%d" % (source, pair), align_bytes=64)
            blocked[source][pair] = tile_in
            for g in range(GROUPS):
                for q in range(4):
                    begin = K_PASS * g + QK * q
                    nc.sync.dma_start(
                        out=tile_in[SQ * q : SQ * (q + 1), g, :, :],
                        in_=(x, hist)[source][first : first + 2 * P, begin : begin + QK].rearrange(
                            "(b j) k -> j b k", j=SQ
                        ),
                    )

        def load_scales(gate, source):
            scale_words = weight_scales[gate][source].bitcast(I32)
            for r in range(4):
                nc.sync.dma_start(
                    out=w_planes[gate][source][4 * (2 * gate + source) + r : P : 32, :, :].bitcast(I32),
                    in_=scale_words[:, r : 16 : 4, :].rearrange("g q n -> q g n"),
                )

        def load_codes(gate, half, sources=(0, 1)):
            for source in sources:
                codes = keep.tile(
                    [P, GROUPS, BANK], U32, name="w_codes_%d_%d_%d" % (gate, source, half), align_bytes=64
                )
                by_partition = weight_words[gate][source].rearrange("g p n t -> p g (n t)")
                nc.sync.dma_start(
                    out=codes[:].bitcast(I32),
                    in_=by_partition[:, :, PACK * BANK * half : PACK * BANK * (half + 1)].bitcast(I32),
                )
                w_codes[gate][source][half] = codes

        load_activations(0)
        for gate in range(2):
            nc.sync.dma_start(out=bias_rows[0:1, gate, :], in_=biases[gate].unsqueeze(0))
        load_activations(1)
        for source in range(2):
            load_scales(0, source)
            load_codes(0, 0, (source,))
        load_activations(2)
        load_codes(0, 1)
        load_blocked(3, 0)
        load_scales(1, 0)
        load_scales(1, 1)
        load_codes(1, 0)
        load_blocked(3, 1)
        load_codes(1, 1)

        a_codes = [[None] * PAIRS for source in range(2)]
        a_planes = [[None] * PAIRS for source in range(2)]

        def transpose_block(source, pair):
            grouped = stage.tile([P, GROUPS, 2, P, PACK], BF16, name="grouped", align_bytes=64)
            for i in range(2):
                words = raw[source][pair][:, i, :].bitcast(F32)
                flipped = psum.tile([P, GROUPS, 2, P], F32, name="flipped", tag="bank")
                for g in range(GROUPS):
                    for u in range(2):
                        nc.tensor.transpose(
                            flipped[:, g, u, :], words[:, WORDS * g + u : WORDS * (g + 1) : 2], identity[:]
                        )
                copy = nc.scalar.copy if i == 0 else nc.vector.tensor_copy
                copy(out=grouped[:, :, i].bitcast(F32), in_=flipped[:].rearrange("p g u r -> p g r u"))
            return grouped

        def order_words(source, pair):
            ordered = stage.tile([P, WORDS_PAIR], F32, name="ordered", align_bytes=64)
            nc.scalar.copy(
                out=ordered[:].rearrange("p (a u w) -> p a u w", u=2, w=SQ),
                in_=blocked[source][pair][:].rearrange("p g b k -> p (g b k)").bitcast(F32).rearrange(
                    "p (a w u) -> p a u w", u=2, w=SQ
                ),
            )
            return ordered

        def turn(ordered):
            turned = stage.tile([P, WORDS_PAIR], F32, name="turned", align_bytes=64)
            nc.vector.transpose(out=turned[:], in_=ordered[:])
            return turned

        def interleave(turned):
            grouped = stage.tile([P, GROUPS, 2, P, PACK], BF16, name="grouped", align_bytes=64)
            nc.scalar.copy(
                out=grouped[:].rearrange("p g i r t -> p (g i r t)").bitcast(F32).rearrange(
                    "p (a j u) -> p a j u", u=2, j=SQ
                ),
                in_=turned[:].rearrange("p (a u j) -> p a j u", u=2, j=SQ),
            )
            return grouped

        def quantise_block(source, pair, grouped):
            a_codes[source][pair] = keep.tile(
                [P, GROUPS, 2, P], U32, name="a_codes_%d_%d" % (source, pair), align_bytes=64
            )
            a_planes[source][pair] = keep.tile(
                [P, GROUPS, 2, P], U8, name="a_planes_%d_%d" % (source, pair), align_bytes=64
            )
            nc.vector.quantize_mx(
                out=a_codes[source][pair][:].rearrange("p g i r -> p (g i r)").bitcast(FP8X4),
                scales=a_planes[source][pair][:].rearrange("p g i r -> p (g i r)"),
                in_=grouped[:].rearrange("p g i r t -> p (g i r t)"),
            )

        bias_all = keep.tile([P, 2, N_OUT], F32, name="bias_all")

        def spread_bias(gate):
            for half in range(HALVES):
                columns = slice(BANK * half, BANK * (half + 1))
                spread = psum.tile([P, BANK], F32, name="spread", tag="bank")
                nc.tensor.matmul(
                    spread[:], lhsT=ones[:, 0:P], rhs=bias_rows[:, gate, columns], start=True, stop=True
                )
                copy = nc.scalar.copy if half == 0 else nc.vector.tensor_copy
                copy(out=bias_all[:, gate, columns], in_=spread[:])

        def gate_values(half, gate, pair, members, between_sources=None):
            columns = slice(BANK * half, BANK * (half + 1))
            accs = {}
            for i in members:
                acc = psum.tile([P, BANK], F32, name="acc", tag="bank")
                accs[i] = acc
            for source in range(2):
                if source == 1 and between_sources is not None:
                    between_sources()
                for i in members:
                    for g in range(GROUPS):
                        nc.tensor.matmul_mx(
                            out=accs[i][:],
                            lhsT=a_codes[source][pair][:, g, i, :].bitcast(FP8X4),
                            lhsT_scale=a_planes[source][pair][:, g, i, :],
                            rhs=w_codes[gate][source][half][:, g, :].bitcast(FP8X4),
                            rhs_scale=w_planes[gate][source][4 * (2 * gate + source) : P, g, columns],
                            start=(source == 0 and g == 0),
                            stop=(source == 1 and g == GROUPS - 1),
                        )
            pair_values = {}
            for i in members:
                values = gates.tile([P, BANK], F32, name="values_%d" % gate)
                pair_values[i] = values
            for i in members:
                nc.vector.tensor_tensor(out=pair_values[i][:], in0=accs[i][:], in1=bias_all[:, gate, columns], op=ALU.add)
            for i in members:
                nc.scalar.activation(out=pair_values[i][:], in_=pair_values[i][:], func=gate_function[gate])
            return pair_values

        def split_candidates(half, pair, i):
            values = gates.tile([P, BANK], F32, name="values_1")
            for inner in pieces:
                columns = slice(BANK * half + inner.start, BANK * half + inner.stop)
                acc = psum.tile([P, BANK], F32, name="acc", tag="bank")
                for source in range(2):
                    for g in range(GROUPS):
                        nc.tensor.matmul_mx(
                            out=acc[:, 0 : inner.stop - inner.start],
                            lhsT=a_codes[source][pair][:, g, i, :].bitcast(FP8X4),
                            lhsT_scale=a_planes[source][pair][:, g, i, :],
                            rhs=w_codes[1][source][half][:, g, inner].bitcast(FP8X4),
                            rhs_scale=w_planes[1][source][4 * (2 + source) : P, g, columns],
                            start=(source == 0 and g == 0),
                            stop=(source == 1 and g == GROUPS - 1),
                        )
                nc.vector.tensor_tensor(
                    out=values[:, inner], in0=acc[:, 0 : inner.stop - inner.start], in1=bias_all[:, 1, columns], op=ALU.add
                )
                nc.scalar.activation(out=values[:, inner], in_=values[:, inner], func=gate_function[1])
            return values

        def store_products(engine, half, pair, input_gates, candidates, spans):
            for i in sorted(candidates):
                for inner in spans:
                    engine.tensor_tensor(
                        out=candidates[i][:, inner], in0=input_gates[i][:, inner], in1=candidates[i][:, inner], op=ALU.mult
                    )
                    nc.sync.dma_start(
                        out=out_rows(2 * pair + i)[:, BANK * half + inner.start : BANK * half + inner.stop],
                        in_=candidates[i][:, inner],
                    )

        def keep_busy(count):
            idle = psum.tile([P, BANK], F32, name="idle", tag="bank")
            for n in range(count):
                nc.tensor.matmul(idle[:], lhsT=ones[:, 0:P], rhs=ones[:], start=True, stop=True)

        keep_busy(WARM_UP)
        grouped_x = transpose_block(0, 0)
        spread_bias(0)
        grouped_h = transpose_block(1, 0)
        quantise_block(0, 0, grouped_x)
        spread_bias(1)
        grouped_x = transpose_block(0, 1)
        quantise_block(1, 0, grouped_h)
        keep_busy(2)
        grouped_h = transpose_block(1, 1)
        quantise_block(0, 1, grouped_x)
        quantise_block(1, 1, grouped_h)

        jobs = [(0, 0, 0), (0, 0, 1), (1, 0, 0), (0, 0, 2), (1, 0, 1), (1, 0, 2)]
        for half in range(HALVES):
            for pair in (0, 1, 2):
                jobs.append((half, 1, pair))
        for gate in range(2):
            jobs.append((0, gate, 3))

        whole = [slice(0, BANK)]
        pieces = [slice(0, BANK // 2), slice(BANK // 2, 3 * BANK // 4), slice(3 * BANK // 4, BANK)]
        input_gates = {}
        steps = {}
        finished = None

        def third_x():
            quantise_block(0, 2, transpose_block(0, 2))

        for index, (half, gate, pair) in enumerate(jobs):
            values = gate_values(half, gate, pair, (0, 1), third_x if index == 1 else None)
            if finished is not None:
                store_products(nc.gpsimd if index in (9, 11, 12) else nc.vector, *finished, whole)
                finished = None
            if gate == 0:
                input_gates[(half, pair)] = values
            else:
                finished = (half, pair, input_gates[(half, pair)], values)
            if index == 1:
                quantise_block(1, 2, transpose_block(1, 2))
            for source, begin in enumerate((3, 6)):
                if index == begin:
                    steps[source] = order_words(source, 3)
                if index == begin + 1:
                    steps[source] = interleave(turn(steps[source]))
                if index == begin + 2:
                    quantise_block(source, 3, steps[source])
        half, pair = HALVES - 1, PAIRS - 1
        first_gates = gate_values(half, 0, pair, (0,))
        products_half, products_pair, products_gates, candidates = finished
        for engine, i in ((nc.gpsimd, 0), (nc.vector, 1)):
            store_products(engine, products_half, products_pair, products_gates, {i: candidates[i]}, whole)
        first = gate_values(half, 1, pair, (0,))
        second_gates = gate_values(half, 0, pair, (1,))
        second = split_candidates(half, pair, 1)
        store_products(nc.vector, half, pair, first_gates, first, whole)
        store_products(nc.vector, half, pair, second_gates, {1: second}, pieces)
